import numpy as np
import ml_dtypes


def mxq(x, axis, fmt="e4m3"):
    dtype, down = {"e4m3": (ml_dtypes.float8_e4m3fn, 7), "e5m2": (ml_dtypes.float8_e5m2, 14)}[fmt]
    v = np.moveaxis(np.asarray(x, np.float32).astype(ml_dtypes.bfloat16).astype(np.float64), axis, -1)
    blocks = v.reshape(v.shape[:-1] + (-1, 32))
    amax = np.abs(blocks).max(-1, keepdims=True)
    byte = np.maximum(np.where(amax > 0, np.frexp(amax)[1] - 1 + 127, 0) - down, 1)
    scale = np.exp2(byte - 127.0)
    codes = (blocks / scale).astype(np.float32).astype(dtype).astype(np.float64)
    return np.moveaxis((codes * scale).reshape(v.shape), -1, axis)


WIDE = False


def mx_kscale(k):
    if not WIDE:
        return np.ones(k)
    levels = np.array([10, -10, 5, -5, 0])
    if k % 512:
        return np.exp2(np.random.permutation(np.resize(levels, k // 32))).repeat(32)
    a = np.empty((k // 512, 16))
    for p in range(k // 512):
        a[p, :8] = np.random.permutation(np.resize(levels, 8))
        for g in range(8):
            far = levels[np.abs(levels - a[p, g]) >= 10]
            a[p, g + 8] = far[np.random.randint(len(far))]
    return np.exp2(a.ravel()).repeat(32)


BF16 = ml_dtypes.bfloat16


def bf(x):
    return np.asarray(x, np.float32).astype(BF16)


def f64(x):
    return np.asarray(x).astype(np.float64)


B, C_IN, H, W, N_HID, N_CLS = 4096, 1, 32, 32, 1024, 128
D = C_IN * H * W
EPS = 1e-12
BN_EPS = 1e-5


def unit_rows(v):
    return v / (np.sqrt((v * v).sum(axis=1, keepdims=True)) + EPS)


def batchnorm(c, gamma, beta):
    mu = c.mean(axis=0)
    var = c.var(axis=0)
    return (c - mu) * (1.0 / np.sqrt(var + BN_EPS)) * gamma + beta


def setup_inputs():
    s = mx_kscale(D)
    r = np.sqrt(np.mean(s * s) * np.mean(1.0 / (s * s)))
    v = (0.5 - 0.5 / np.pi) / D
    comp = np.exp2(np.round(np.log2(r * np.sqrt((v / (r * r) + BN_EPS) / (v + BN_EPS)))))
    contrast = np.exp2(np.random.uniform(-1.0, 1.0, B))[:, None, None, None]
    length = np.exp2(np.random.uniform(-3.0, 0.0, N_HID))[:, None]
    return {"x": bf(np.random.standard_normal((B, C_IN, H, W)) * contrast * s.reshape(C_IN, H, W)),
            "w1": bf(np.random.standard_normal((N_HID, D)) * length / np.sqrt(D) / s[None, :]),
            "g1": bf((1.0 + 0.1 * np.random.standard_normal(N_HID)) * comp),
            "b1": bf(0.1 * np.random.standard_normal(N_HID))}


def reference(x, w1, g1, b1):
    xf = f64(x).reshape(B, -1)
    xn = unit_rows(xf)
    wn = unit_rows(f64(w1))
    c = np.clip(mxq(xn, 1, "e4m3") @ mxq(wn, 1, "e4m3").T, 0.0, 1.0)
    return batchnorm(c, f64(g1), f64(b1))

@@ -1,0 +1,291 @@
+from contextlib import ExitStack
+
+import concourse.mybir as mybir
+from concourse.masks import make_identity
+
+F32 = mybir.dt.float32
+BF16 = mybir.dt.bfloat16
+U32 = mybir.dt.uint32
+U8 = mybir.dt.uint8
+FP8X4 = mybir.dt.float8_e4m3fn_x4
+ALU = mybir.AluOpType
+ACT = mybir.ActivationFunctionType
+AXIS = mybir.AxisListType
+
+P = 128
+BATCH = 4096
+K = 1024
+CHANNELS = 1024
+EPS = 1e-12
+BN_EPS = 1e-5
+
+PACK = 4
+PASSES = K // (P * PACK)
+WORDS = K // 2
+BANK_TILES = 4
+COLS = BANK_TILES * P
+
+GROUP = BANK_TILES
+X_TILES = BATCH // P
+X_GROUPS = BATCH // COLS
+W_GROUPS = CHANNELS // COLS
+GROUPS = W_GROUPS + X_GROUPS
+LOAD_AHEAD = 4
+
+PAIR = 2
+C_TILES = CHANNELS // P
+STEP_GROUPS = 2
+STEP_COLS = STEP_GROUPS * COLS
+STEP_TILES = STEP_COLS // P
+PAIR_STEPS = BATCH // STEP_COLS
+STEPS = (C_TILES // PAIR) * PAIR_STEPS
+LAG = PAIR_STEPS + 1
+
+FLOPS = 2 * BATCH * K * CHANNELS
+
+
+def tile_net_pa_t_kernel(tc, x, w1, g1, b1, out):
+    nc = tc.nc
+    x_rows = x.rearrange("(p t) c h w -> p t (c h w)", t=X_TILES)
+    out_rows = out.rearrange("(p t) j -> p t j", t=X_TILES)
+    w_rows = w1.rearrange("(t p) k -> p t k", p=P)
+
+    with ExitStack() as stack:
+        const = stack.enter_context(tc.tile_pool(name="const", bufs=1))
+        small = stack.enter_context(tc.tile_pool(name="small", bufs=4))
+        scratch = stack.enter_context(tc.tile_pool(name="scratch", bufs=4))
+        load_pool = stack.enter_context(tc.tile_pool(name="load", bufs=LOAD_AHEAD + 1))
+        prep_pool = stack.enter_context(tc.tile_pool(name="prep", bufs=2))
+        sims_pool = stack.enter_context(tc.tile_pool(name="sims", bufs=LAG + 2))
+        stage_pool = stack.enter_context(tc.tile_pool(name="stage", bufs=3))
+        turn_pool = stack.enter_context(tc.psum_pool(name="turn", bufs=4))
+        product_pool = stack.enter_context(tc.psum_pool(name="product", bufs=4))
+
+        warm = const.tile([P, 1], F32)
+        nc.vector.memset(warm[:], 1.0)
+        nc.scalar.sqrt(out=warm[:], in_=warm[:])
+
+        identity = const.tile([P, P], F32)
+        make_identity(nc, identity[:])
+        identity_bf16 = const.tile([P, P], BF16)
+        make_identity(nc, identity_bf16[:])
+        ones = const.tile([P, COLS], F32)
+        nc.vector.memset(ones[:], 1.0)
+        gain_shift_rows = const.tile([P, P], BF16)
+        nc.gpsimd.memset(gain_shift_rows[:], 0.0)
+
+        w_codes = const.tile([P, PASSES, CHANNELS], U32, align_bytes=64)
+        w_scales = const.tile([P, PASSES, CHANNELS], U8, align_bytes=64)
+        x_codes = const.tile([P, PASSES, BATCH], U32, align_bytes=64)
+        x_scales = const.tile([P, PASSES, BATCH], U8, align_bytes=64)
+
+        group_rows, group_codes, group_scales = [], [], []
+        for rows, codes, scales, count in (
+            (w_rows, w_codes, w_scales, W_GROUPS),
+            (x_rows, x_codes, x_scales, X_GROUPS),
+        ):
+            for n in range(count):
+                group_rows.append(rows[:, n * GROUP : (n + 1) * GROUP, :])
+                group_codes.append(codes[:, :, n * COLS : (n + 1) * COLS])
+                group_scales.append(scales[:, :, n * COLS : (n + 1) * COLS])
+
+        raw, norm, inverse, grouped, turned = {}, {}, {}, {}, {}
+
+        def load(m):
+            raw[m] = load_pool.tile([P, GROUP, K], BF16, name="raw")
+            for i in range(GROUP):
+                nc.sync.dma_start(out=raw[m][:, i, :], in_=group_rows[m][:, i, :])
+
+        def row_norms(m):
+            sumsq = small.tile([P, GROUP], F32)
+            for i in range(GROUP):
+                squares = scratch.tile([P, K], BF16)
+                nc.scalar.activation(
+                    out=squares[:], in_=raw[m][:, i, :], func=ACT.Square,
+                    accum_out=sumsq[:, i : i + 1],
+                )
+            norm[m] = small.tile([P, GROUP], F32, name="norm")
+            nc.scalar.sqrt(out=norm[m][:], in_=sumsq[:])
+
+        def invert(m):
+            nc.vector.tensor_scalar(
+                out=norm[m][:], in0=norm[m][:], scalar1=0.0, scalar2=EPS, op0=ALU.max, op1=ALU.add
+            )
+            inverse[m] = small.tile([P, GROUP], F32, name="inverse")
+            nc.vector.reciprocal(out=inverse[m][:], in_=norm[m][:])
+
+        def turn(m):
+            unit = prep_pool.tile([P, GROUP * K], BF16)
+            unit_words = unit[:].bitcast(F32)
+            for i in range(GROUP):
+                nc.vector.tensor_scalar_mul(
+                    out=unit[:, i * K : (i + 1) * K], in0=raw[m][:, i, :],
+                    scalar1=inverse[m][:, i : i + 1],
+                )
+                turned[m, i] = turn_pool.tile([P, PASSES * 2, P], F32, name="turned", tag="turn")
+                for s in range(PASSES * 2):
+                    g, u = divmod(s, 2)
+                    first = i * WORDS + g * 2 * P + u
+                    nc.tensor.transpose(
+                        turned[m, i][:, s, :],
+                        unit_words[:, first : i * WORDS + (g + 1) * 2 * P : 2],
+                        identity[:],
+                    )
+
+        def regroup(m):
+            grouped[m] = prep_pool.tile(
+                [P, PASSES * COLS * PACK], BF16, name="grouped", align_bytes=64
+            )
+            words = grouped[m][:].bitcast(F32).rearrange("p (g c u) -> p g c u", g=PASSES, u=2)
+            for i in range(GROUP):
+                copy = nc.scalar.copy if i == GROUP - 1 else nc.vector.tensor_copy
+                copy(
+                    out=words[:, :, i * P : (i + 1) * P, :],
+                    in_=turned[m, i][:].rearrange("p (g u) r -> p g r u", u=2),
+                )
+
+        def quantise(m):
+            for g in range(PASSES):
+                nc.vector.quantize_mx(
+                    out=group_codes[m][:, g, :].bitcast(FP8X4),
+                    scales=group_scales[m][:, g, :],
+                    in_=grouped[m][:, g * COLS * PACK : (g + 1) * COLS * PACK],
+                )
+
+        for m in range(-LOAD_AHEAD, GROUPS + 1):
+            if 0 <= m + LOAD_AHEAD < GROUPS:
+                load(m + LOAD_AHEAD)
+            if 0 <= m < GROUPS:
+                turn(m)
+            if 0 <= m - 1 < GROUPS:
+                quantise(m - 1)
+            if 0 <= m < GROUPS:
+                regroup(m)
+            if 0 <= m + 1 < GROUPS:
+                invert(m + 1)
+            if 0 <= m + 2 < GROUPS:
+                row_norms(m + 2)
+
+        nc.sync.dma_start(out=gain_shift_rows[0:C_TILES, :], in_=g1.rearrange("(t p) -> t p", p=P))
+        nc.sync.dma_start(
+            out=gain_shift_rows[C_TILES : 2 * C_TILES, :], in_=b1.rearrange("(t p) -> t p", p=P)
+        )
+        gain_shift_turned = turn_pool.tile([P, P], BF16, tag="turn")
+        nc.tensor.transpose(gain_shift_turned[:], gain_shift_rows[:], identity_bf16[:])
+        gain_shift = const.tile([P, 2 * C_TILES], F32)
+        nc.vector.tensor_copy(out=gain_shift[:], in_=gain_shift_turned[:, 0 : 2 * C_TILES])
+
+        sims, partial, sums, spread, lever, scale, offset = {}, {}, {}, {}, {}, {}, {}
+
+        def similarities(k):
+            u, q = divmod(k, PAIR_STEPS)
+            if q == 0:
+                partial[u] = small.tile([P, 2, PAIR, X_GROUPS], F32, name="partial")
+            sims[k] = sims_pool.tile([P, PAIR, STEP_COLS], F32, name="sims")
+            for h in range(STEP_GROUPS):
+                n = q * STEP_GROUPS + h
+                cols = slice(n * COLS, (n + 1) * COLS)
+                for j in range(PAIR):
+                    channels = slice((u * PAIR + j) * P, (u * PAIR + j + 1) * P)
+                    product = product_pool.tile([P, COLS], F32)
+                    for g in range(PASSES):
+                        nc.tensor.matmul_mx(
+                            out=product[:],
+                            lhsT=w_codes[:, g, channels].bitcast(FP8X4),
+                            lhsT_scale=w_scales[:, g, channels],
+                            rhs=x_codes[:, g, cols].bitcast(FP8X4),
+                            rhs_scale=x_scales[:, g, cols],
+                            start=(g == 0),
+                            stop=(g == PASSES - 1),
+                        )
+                    clipped = sims[k][:, j, h * COLS : (h + 1) * COLS]
+                    nc.vector.scalar_tensor_tensor(
+                        out=clipped, in0=product[:], scalar=0.0, in1=ones[:],
+                        op0=ALU.max, op1=ALU.min, accum_out=partial[u][:, 0, j, n : n + 1],
+                    )
+                    squares = scratch.tile([P, COLS], BF16)
+                    nc.scalar.activation(
+                        out=squares[:], in_=clipped, func=ACT.Square,
+                        accum_out=partial[u][:, 1, j, n : n + 1],
+                    )
+
+        def deviation(u):
+            gain = gain_shift[:, u * PAIR : (u + 1) * PAIR]
+            sums[u] = small.tile([P, 2, PAIR], F32, name="sums")
+            nc.vector.tensor_reduce(out=sums[u][:], in_=partial[u][:], axis=AXIS.X, op=ALU.add)
+            spread[u] = small.tile([P, PAIR], F32, name="spread")
+            nc.vector.tensor_mul(out=spread[u][:], in0=sums[u][:, 0, :], in1=sums[u][:, 0, :])
+            lever[u] = small.tile([P, PAIR], F32, name="lever")
+            nc.vector.scalar_tensor_tensor(
+                out=lever[u][:], in0=sums[u][:, 0, :], scalar=-1.0 / BATCH, in1=gain,
+                op0=ALU.mult, op1=ALU.mult,
+            )
+            nc.vector.scalar_tensor_tensor(
+                out=spread[u][:], in0=spread[u][:], scalar=-1.0 / BATCH, in1=sums[u][:, 1, :],
+                op0=ALU.mult, op1=ALU.add,
+            )
+            nc.vector.tensor_scalar(
+                out=spread[u][:], in0=spread[u][:], scalar1=0.0, scalar2=BATCH * BN_EPS,
+                op0=ALU.max, op1=ALU.add,
+            )
+            nc.scalar.activation(
+                out=spread[u][:], in_=spread[u][:], func=ACT.Sqrt, scale=1.0 / BATCH
+            )
+
+        def scale_and_offset(u):
+            gain = gain_shift[:, u * PAIR : (u + 1) * PAIR]
+            inverse_deviation = small.tile([P, PAIR], F32)
+            nc.vector.reciprocal(out=inverse_deviation[:], in_=spread[u][:])
+            scale[u] = small.tile([P, PAIR], F32, name="scale")
+            nc.vector.tensor_mul(out=scale[u][:], in0=inverse_deviation[:], in1=gain)
+            offset[u] = small.tile([P, PAIR], F32, name="offset")
+            for j in range(PAIR):
+                t = u * PAIR + j
+                nc.vector.scalar_tensor_tensor(
+                    out=offset[u][:, j : j + 1], in0=lever[u][:, j : j + 1],
+                    scalar=inverse_deviation[:, j : j + 1],
+                    in1=gain_shift[:, C_TILES + t : C_TILES + t + 1], op0=ALU.mult, op1=ALU.add,
+                )
+
+        def normalise(k):
+            u = k // PAIR_STEPS
+            nc.gpsimd.tensor_scalar(
+                out=sims[k][:, 0, :], in0=sims[k][:, 0, :],
+                scalar1=scale[u][:, 0:1], scalar2=offset[u][:, 0:1], op0=ALU.mult, op1=ALU.add,
+            )
+            nc.vector.tensor_scalar(
+                out=sims[k][:, 1, :], in0=sims[k][:, 1, :],
+                scalar1=scale[u][:, 1:2], scalar2=offset[u][:, 1:2], op0=ALU.mult, op1=ALU.add,
+            )
+
+        def turn_back(k):
+            u, q = divmod(k, PAIR_STEPS)
+            stage = stage_pool.tile([P, STEP_TILES, PAIR * P], F32)
+            for b in range(STEP_TILES // 2):
+                flipped = turn_pool.tile([P, 2, PAIR, P], F32, tag="turn")
+                for i in range(2):
+                    images = slice((2 * b + i) * P, (2 * b + i + 1) * P)
+                    for j in range(PAIR):
+                        nc.tensor.transpose(flipped[:, i, j, :], sims[k][:, j, images], identity[:])
+                staged = stage[:, 2 * b : 2 * b + 2, :]
+                if b == 0:
+                    nc.vector.tensor_copy(out=staged, in_=flipped[:].rearrange("p i j c -> p i (j c)"))
+                else:
+                    nc.scalar.copy(out=staged, in_=flipped[:].rearrange("p i j c -> p i (j c)"))
+            nc.sync.dma_start(
+                out=out_rows[:, q * STEP_TILES : (q + 1) * STEP_TILES, u * PAIR * P : (u + 1) * PAIR * P],
+                in_=stage[:],
+            )
+
+        for k in range(STEPS + LAG):
+            pair_done = k % PAIR_STEPS == 0 and k > 0 and k <= STEPS
+            if k < STEPS:
+                similarities(k)
+            if pair_done:
+                deviation(k // PAIR_STEPS - 1)
+            if k >= LAG:
+                turn_back(k - LAG)
+            if pair_done:
+                scale_and_offset(k // PAIR_STEPS - 1)
+            if 0 <= k - LAG + 1 < STEPS:
+                normalise(k - LAG + 1)

@@ -249,14 +249,12 @@ def tile_net_pa_t_kernel(tc, x, w1, g1, b1, out):
 
         def normalise(k):
             u = k // PAIR_STEPS
-            nc.gpsimd.tensor_scalar(
-                out=sims[k][:, 0, :], in0=sims[k][:, 0, :],
-                scalar1=scale[u][:, 0:1], scalar2=offset[u][:, 0:1], op0=ALU.mult, op1=ALU.add,
-            )
-            nc.vector.tensor_scalar(
-                out=sims[k][:, 1, :], in0=sims[k][:, 1, :],
-                scalar1=scale[u][:, 1:2], scalar2=offset[u][:, 1:2], op0=ALU.mult, op1=ALU.add,
-            )
+            for j in range(PAIR):
+                nc.vector.tensor_scalar(
+                    out=sims[k][:, j, :], in0=sims[k][:, j, :],
+                    scalar1=scale[u][:, j : j + 1], scalar2=offset[u][:, j : j + 1],
+                    op0=ALU.mult, op1=ALU.add,
+                )
 
         def turn_back(k):
             u, q = divmod(k, PAIR_STEPS)

@@ -100,10 +100,16 @@ def tile_net_pa_t_kernel(tc, x, w1, g1, b1, out):
             sumsq = small.tile([P, GROUP], F32)
             for i in range(GROUP):
                 squares = scratch.tile([P, K], BF16)
-                nc.scalar.activation(
-                    out=squares[:], in_=raw[m][:, i, :], func=ACT.Square,
-                    accum_out=sumsq[:, i : i + 1],
-                )
+                if m == 0 and i % 2 == 1:
+                    nc.vector.scalar_tensor_tensor(
+                        out=squares[:], in0=raw[m][:, i, :], scalar=1.0, in1=raw[m][:, i, :],
+                        op0=ALU.mult, op1=ALU.mult, accum_out=sumsq[:, i : i + 1],
+                    )
+                else:
+                    nc.scalar.activation(
+                        out=squares[:], in_=raw[m][:, i, :], func=ACT.Square,
+                        accum_out=sumsq[:, i : i + 1],
+                    )
             norm[m] = small.tile([P, GROUP], F32, name="norm")
             nc.scalar.sqrt(out=norm[m][:], in_=sumsq[:])
 

@@ -181,7 +181,7 @@ def tile_net_pa_t_kernel(tc, x, w1, g1, b1, out):
         gain_shift = const.tile([P, 2 * C_TILES], F32)
         nc.vector.tensor_copy(out=gain_shift[:], in_=gain_shift_turned[:, 0 : 2 * C_TILES])
 
-        sims, partial, sums, spread, lever, scale, offset = {}, {}, {}, {}, {}, {}, {}
+        sims, partial, sums, spread, scale, offset = {}, {}, {}, {}, {}, {}
 
         def similarities(k):
             u, q = divmod(k, PAIR_STEPS)
@@ -216,47 +216,38 @@ def tile_net_pa_t_kernel(tc, x, w1, g1, b1, out):
                     )
 
         def deviation(u):
-            gain = gain_shift[:, u * PAIR : (u + 1) * PAIR]
+            engine = nc.gpsimd if u < C_TILES // PAIR - 1 else nc.vector
             sums[u] = small.tile([P, 2, PAIR], F32, name="sums")
             nc.vector.tensor_reduce(out=sums[u][:], in_=partial[u][:], axis=AXIS.X, op=ALU.add)
-            spread[u] = small.tile([P, PAIR], F32, name="spread")
-            nc.vector.tensor_mul(out=spread[u][:], in0=sums[u][:, 0, :], in1=sums[u][:, 0, :])
-            lever[u] = small.tile([P, PAIR], F32, name="lever")
-            nc.vector.scalar_tensor_tensor(
-                out=lever[u][:], in0=sums[u][:, 0, :], scalar=-1.0 / BATCH, in1=gain,
-                op0=ALU.mult, op1=ALU.mult,
-            )
-            nc.vector.scalar_tensor_tensor(
-                out=spread[u][:], in0=spread[u][:], scalar=-1.0 / BATCH, in1=sums[u][:, 1, :],
+            engine.tensor_scalar(
+                out=sums[u][:], in0=sums[u][:], scalar1=1.0 / BATCH, scalar2=0.0,
                 op0=ALU.mult, op1=ALU.add,
             )
-            nc.vector.tensor_scalar(
-                out=spread[u][:], in0=spread[u][:], scalar1=0.0, scalar2=BATCH * BN_EPS,
+            spread[u] = small.tile([P, PAIR], F32, name="spread")
+            engine.tensor_mul(out=spread[u][:], in0=sums[u][:, 0, :], in1=sums[u][:, 0, :])
+            engine.tensor_sub(out=spread[u][:], in0=sums[u][:, 1, :], in1=spread[u][:])
+            engine.tensor_scalar(
+                out=spread[u][:], in0=spread[u][:], scalar1=0.0, scalar2=BN_EPS,
                 op0=ALU.max, op1=ALU.add,
             )
-            nc.scalar.activation(
-                out=spread[u][:], in_=spread[u][:], func=ACT.Sqrt, scale=1.0 / BATCH
-            )
+            nc.scalar.sqrt(out=spread[u][:], in_=spread[u][:])
 
         def scale_and_offset(u):
+            engine = nc.gpsimd if u < C_TILES // PAIR - 1 else nc.vector
             gain = gain_shift[:, u * PAIR : (u + 1) * PAIR]
-            inverse_deviation = small.tile([P, PAIR], F32)
-            nc.vector.reciprocal(out=inverse_deviation[:], in_=spread[u][:])
+            shift = gain_shift[:, C_TILES + u * PAIR : C_TILES + (u + 1) * PAIR]
+            nc.vector.reciprocal(out=spread[u][:], in_=spread[u][:])
             scale[u] = small.tile([P, PAIR], F32, name="scale")
-            nc.vector.tensor_mul(out=scale[u][:], in0=inverse_deviation[:], in1=gain)
+            engine.tensor_mul(out=scale[u][:], in0=spread[u][:], in1=gain)
             offset[u] = small.tile([P, PAIR], F32, name="offset")
-            for j in range(PAIR):
-                t = u * PAIR + j
-                nc.vector.scalar_tensor_tensor(
-                    out=offset[u][:, j : j + 1], in0=lever[u][:, j : j + 1],
-                    scalar=inverse_deviation[:, j : j + 1],
-                    in1=gain_shift[:, C_TILES + t : C_TILES + t + 1], op0=ALU.mult, op1=ALU.add,
-                )
+            engine.tensor_mul(out=offset[u][:], in0=sums[u][:, 0, :], in1=scale[u][:])
+            engine.tensor_sub(out=offset[u][:], in0=shift, in1=offset[u][:])
 
         def normalise(k):
             u = k // PAIR_STEPS
+            engine = nc.gpsimd if u < C_TILES // PAIR - 1 else nc.vector
             for j in range(PAIR):
-                nc.vector.tensor_scalar(
+                engine.tensor_scalar(
                     out=sims[k][:, j, :], in0=sims[k][:, j, :],
                     scalar1=scale[u][:, j : j + 1], scalar2=offset[u][:, j : j + 1],
                     op0=ALU.mult, op1=ALU.add,
@@ -272,7 +263,7 @@ def tile_net_pa_t_kernel(tc, x, w1, g1, b1, out):
                     for j in range(PAIR):
                         nc.tensor.transpose(flipped[:, i, j, :], sims[k][:, j, images], identity[:])
                 staged = stage[:, 2 * b : 2 * b + 2, :]
-                if b == 0:
+                if b % 2 == 0:
                     nc.vector.tensor_copy(out=staged, in_=flipped[:].rearrange("p i j c -> p i (j c)"))
                 else:
                     nc.scalar.copy(out=staged, in_=flipped[:].rearrange("p i j c -> p i (j c)"))

@@ -39,7 +39,7 @@ STEP_COLS = STEP_GROUPS * COLS
 STEP_TILES = STEP_COLS // P
 PAIR_STEPS = BATCH // STEP_COLS
 STEPS = (C_TILES // PAIR) * PAIR_STEPS
-LAG = PAIR_STEPS + 1
+LAG = PAIR_STEPS + 3
 
 FLOPS = 2 * BATCH * K * CHANNELS
 
@@ -244,9 +244,15 @@ def tile_net_pa_t_kernel(tc, x, w1, g1, b1, out):
             engine.tensor_sub(out=offset[u][:], in0=shift, in1=offset[u][:])
 
         def normalise(k):
-            u = k // PAIR_STEPS
-            engine = nc.gpsimd if u < C_TILES // PAIR - 1 else nc.vector
+            u, q = divmod(k, PAIR_STEPS)
             for j in range(PAIR):
+                if u == C_TILES // PAIR - 2 and q == PAIR_STEPS - 1:
+                    nc.scalar.activation(
+                        out=sims[k][:, j, :], in_=sims[k][:, j, :], func=ACT.Identity,
+                        scale=scale[u][:, j : j + 1], bias=offset[u][:, j : j + 1],
+                    )
+                    continue
+                engine = nc.gpsimd if u < C_TILES // PAIR - 1 else nc.vector
                 engine.tensor_scalar(
                     out=sims[k][:, j, :], in0=sims[k][:, j, :],
                     scalar1=scale[u][:, j : j + 1], scalar2=offset[u][:, j : j + 1],

@@ -71,6 +71,10 @@ def tile_net_pa_t_kernel(tc, x, w1, g1, b1, out):
         make_identity(nc, identity_bf16[:])
         ones = const.tile([P, COLS], F32)
         nc.vector.memset(ones[:], 1.0)
+        bn_eps = const.tile([P, 1], F32)
+        nc.vector.tensor_scalar(
+            out=bn_eps[:], in0=ones[:, 0:1], scalar1=0.0, scalar2=BN_EPS, op0=ALU.mult, op1=ALU.add
+        )
         gain_shift_rows = const.tile([P, P], BF16)
         nc.gpsimd.memset(gain_shift_rows[:], 0.0)
 
@@ -181,7 +185,7 @@ def tile_net_pa_t_kernel(tc, x, w1, g1, b1, out):
         gain_shift = const.tile([P, 2 * C_TILES], F32)
         nc.vector.tensor_copy(out=gain_shift[:], in_=gain_shift_turned[:, 0 : 2 * C_TILES])
 
-        sims, partial, sums, spread, scale, offset = {}, {}, {}, {}, {}, {}
+        sims, partial, sums, minus_mean, spread, scale, offset = {}, {}, {}, {}, {}, {}, {}
 
         def similarities(k):
             u, q = divmod(k, PAIR_STEPS)
@@ -216,32 +220,43 @@ def tile_net_pa_t_kernel(tc, x, w1, g1, b1, out):
                     )
 
         def deviation(u):
-            engine = nc.gpsimd if u < C_TILES // PAIR - 1 else nc.vector
             sums[u] = small.tile([P, 2, PAIR], F32, name="sums")
             nc.vector.tensor_reduce(out=sums[u][:], in_=partial[u][:], axis=AXIS.X, op=ALU.add)
-            engine.tensor_scalar(
-                out=sums[u][:], in0=sums[u][:], scalar1=1.0 / BATCH, scalar2=0.0,
-                op0=ALU.mult, op1=ALU.add,
+            minus_mean[u] = small.tile([P, PAIR], F32, name="minus_mean")
+            nc.scalar.activation(
+                out=minus_mean[u][:], in_=sums[u][:, 0, :], func=ACT.Copy, scale=-1.0 / BATCH
+            )
+            squared_sum = small.tile([P, PAIR], F32)
+            nc.scalar.activation(
+                out=squared_sum[:], in_=sums[u][:, 0, :], func=ACT.Square, scale=BATCH**-0.5
             )
             spread[u] = small.tile([P, PAIR], F32, name="spread")
-            engine.tensor_mul(out=spread[u][:], in0=sums[u][:, 0, :], in1=sums[u][:, 0, :])
-            engine.tensor_sub(out=spread[u][:], in0=sums[u][:, 1, :], in1=spread[u][:])
-            engine.tensor_scalar(
-                out=spread[u][:], in0=spread[u][:], scalar1=0.0, scalar2=BN_EPS,
-                op0=ALU.max, op1=ALU.add,
+            for j in range(PAIR):
+                nc.scalar.activation(
+                    out=spread[u][:, j : j + 1], in_=squared_sum[:, j : j + 1], func=ACT.Relu,
+                    scale=-1.0, bias=sums[u][:, 1, j : j + 1],
+                )
+            nc.scalar.activation(
+                out=spread[u][:], in_=spread[u][:], func=ACT.Sqrt, scale=1.0 / BATCH, bias=bn_eps[:]
             )
-            nc.scalar.sqrt(out=spread[u][:], in_=spread[u][:])
 
         def scale_and_offset(u):
-            engine = nc.gpsimd if u < C_TILES // PAIR - 1 else nc.vector
-            gain = gain_shift[:, u * PAIR : (u + 1) * PAIR]
-            shift = gain_shift[:, C_TILES + u * PAIR : C_TILES + (u + 1) * PAIR]
             nc.vector.reciprocal(out=spread[u][:], in_=spread[u][:])
             scale[u] = small.tile([P, PAIR], F32, name="scale")
-            engine.tensor_mul(out=scale[u][:], in0=spread[u][:], in1=gain)
             offset[u] = small.tile([P, PAIR], F32, name="offset")
-            engine.tensor_mul(out=offset[u][:], in0=sums[u][:, 0, :], in1=scale[u][:])
-            engine.tensor_sub(out=offset[u][:], in0=shift, in1=offset[u][:])
+            for j in range(PAIR):
+                t = u * PAIR + j
+                nc.scalar.activation(
+                    out=scale[u][:, j : j + 1], in_=gain_shift[:, t : t + 1], func=ACT.Copy,
+                    scale=spread[u][:, j : j + 1],
+                )
+            for j in range(PAIR):
+                t = u * PAIR + j
+                nc.scalar.activation(
+                    out=offset[u][:, j : j + 1], in_=scale[u][:, j : j + 1], func=ACT.Identity,
+                    scale=minus_mean[u][:, j : j + 1],
+                    bias=gain_shift[:, C_TILES + t : C_TILES + t + 1],
+                )
 
         def normalise(k):
             u, q = divmod(k, PAIR_STEPS)
@@ -283,10 +298,10 @@ def tile_net_pa_t_kernel(tc, x, w1, g1, b1, out):
             if k < STEPS:
                 similarities(k)
             if pair_done:
-                deviation(k // PAIR_STEPS - 1)
+                with tc.high_priority():
+                    deviation(k // PAIR_STEPS - 1)
+                    scale_and_offset(k // PAIR_STEPS - 1)
             if k >= LAG:
                 turn_back(k - LAG)
-            if pair_done:
-                scale_and_offset(k // PAIR_STEPS - 1)
             if 0 <= k - LAG + 1 < STEPS:
                 normalise(k - LAG + 1)

@@ -267,7 +267,7 @@ def tile_net_pa_t_kernel(tc, x, w1, g1, b1, out):
                         scale=scale[u][:, j : j + 1], bias=offset[u][:, j : j + 1],
                     )
                     continue
-                engine = nc.gpsimd if u < C_TILES // PAIR - 1 else nc.vector
+                engine = nc.gpsimd if 0 < k < STEPS - PAIR_STEPS else nc.vector
                 engine.tensor_scalar(
                     out=sims[k][:, j, :], in0=sims[k][:, j, :],
                     scalar1=scale[u][:, j : j + 1], scalar2=offset[u][:, j : j + 1],
@@ -288,10 +288,15 @@ def tile_net_pa_t_kernel(tc, x, w1, g1, b1, out):
                     nc.vector.tensor_copy(out=staged, in_=flipped[:].rearrange("p i j c -> p i (j c)"))
                 else:
                     nc.scalar.copy(out=staged, in_=flipped[:].rearrange("p i j c -> p i (j c)"))
-            nc.sync.dma_start(
-                out=out_rows[:, q * STEP_TILES : (q + 1) * STEP_TILES, u * PAIR * P : (u + 1) * PAIR * P],
-                in_=stage[:],
-            )
+                if b % 2 == 1:
+                    tiles = slice(2 * b - 2, 2 * b + 2)
+                    nc.sync.dma_start(
+                        out=out_rows[
+                            :, q * STEP_TILES + 2 * b - 2 : q * STEP_TILES + 2 * b + 2,
+                            u * PAIR * P : (u + 1) * PAIR * P,
+                        ],
+                        in_=stage[:, tiles, :],
+                    )
 
         for k in range(STEPS + LAG):
             pair_done = k % PAIR_STEPS == 0 and k > 0 and k <= STEPS
@@ -301,7 +306,10 @@ def tile_net_pa_t_kernel(tc, x, w1, g1, b1, out):
                 with tc.high_priority():
                     deviation(k // PAIR_STEPS - 1)
                     scale_and_offset(k // PAIR_STEPS - 1)
-            if k >= LAG:
+                    if k == PAIR_STEPS:
+                        normalise(0)
+                        turn_back(0)
+            if k > LAG:
                 turn_back(k - LAG)
-            if 0 <= k - LAG + 1 < STEPS:
+            if 0 < k - LAG + 1 < STEPS:
                 normalise(k - LAG + 1)

@@ -129,16 +129,17 @@ def tile_net_pa_t_kernel(tc, x, w1, g1, b1, out):
             unit_words = unit[:].bitcast(F32)
             for i in range(GROUP):
                 nc.vector.tensor_scalar_mul(
-                    out=unit[:, i * K : (i + 1) * K], in0=raw[m][:, i, :],
+                    out=unit[:, i * K : (i + 1) * K].rearrange("p (u c e) -> p u c e", u=2, e=2),
+                    in0=raw[m][:, i, :].rearrange("p (c u e) -> p u c e", u=2, e=2),
                     scalar1=inverse[m][:, i : i + 1],
                 )
                 turned[m, i] = turn_pool.tile([P, PASSES * 2, P], F32, name="turned", tag="turn")
                 for s in range(PASSES * 2):
                     g, u = divmod(s, 2)
-                    first = i * WORDS + g * 2 * P + u
+                    first = i * WORDS + (u * PASSES + g) * P
                     nc.tensor.transpose(
                         turned[m, i][:, s, :],
-                        unit_words[:, first : i * WORDS + (g + 1) * 2 * P : 2],
+                        unit_words[:, first : first + P],
                         identity[:],
                     )
 

from contextlib import ExitStack

import concourse.mybir as mybir
from concourse.masks import make_identity

F32 = mybir.dt.float32
BF16 = mybir.dt.bfloat16
U32 = mybir.dt.uint32
U8 = mybir.dt.uint8
FP8X4 = mybir.dt.float8_e4m3fn_x4
ALU = mybir.AluOpType
ACT = mybir.ActivationFunctionType
AXIS = mybir.AxisListType

P = 128
BATCH = 4096
K = 1024
CHANNELS = 1024
EPS = 1e-12
BN_EPS = 1e-5

PACK = 4
PASSES = K // (P * PACK)
WORDS = K // 2
BANK_TILES = 4
COLS = BANK_TILES * P

GROUP = BANK_TILES
X_TILES = BATCH // P
X_GROUPS = BATCH // COLS
W_GROUPS = CHANNELS // COLS
GROUPS = W_GROUPS + X_GROUPS
LOAD_AHEAD = 4

PAIR = 2
C_TILES = CHANNELS // P
STEP_GROUPS = 2
STEP_COLS = STEP_GROUPS * COLS
STEP_TILES = STEP_COLS // P
PAIR_STEPS = BATCH // STEP_COLS
STEPS = (C_TILES // PAIR) * PAIR_STEPS
LAG = PAIR_STEPS + 3

FLOPS = 2 * BATCH * K * CHANNELS


def tile_net_pa_t_kernel(tc, x, w1, g1, b1, out):
    nc = tc.nc
    x_rows = x.rearrange("(p t) c h w -> p t (c h w)", t=X_TILES)
    out_rows = out.rearrange("(p t) j -> p t j", t=X_TILES)
    w_rows = w1.rearrange("(t p) k -> p t k", p=P)

    with ExitStack() as stack:
        const = stack.enter_context(tc.tile_pool(name="const", bufs=1))
        small = stack.enter_context(tc.tile_pool(name="small", bufs=4))
        scratch = stack.enter_context(tc.tile_pool(name="scratch", bufs=4))
        load_pool = stack.enter_context(tc.tile_pool(name="load", bufs=LOAD_AHEAD + 1))
        prep_pool = stack.enter_context(tc.tile_pool(name="prep", bufs=2))
        sims_pool = stack.enter_context(tc.tile_pool(name="sims", bufs=LAG + 2))
        stage_pool = stack.enter_context(tc.tile_pool(name="stage", bufs=3))
        turn_pool = stack.enter_context(tc.psum_pool(name="turn", bufs=4))
        product_pool = stack.enter_context(tc.psum_pool(name="product", bufs=4))

        warm = const.tile([P, 1], F32)
        nc.vector.memset(warm[:], 1.0)
        nc.scalar.sqrt(out=warm[:], in_=warm[:])

        identity = const.tile([P, P], F32)
        make_identity(nc, identity[:])
        identity_bf16 = const.tile([P, P], BF16)
        make_identity(nc, identity_bf16[:])
        ones = const.tile([P, COLS], F32)
        nc.vector.memset(ones[:], 1.0)
        bn_eps = const.tile([P, 1], F32)
        nc.vector.tensor_scalar(
            out=bn_eps[:], in0=ones[:, 0:1], scalar1=0.0, scalar2=BN_EPS, op0=ALU.mult, op1=ALU.add
        )
        gain_shift_rows = const.tile([P, P], BF16)
        nc.gpsimd.memset(gain_shift_rows[:], 0.0)

        w_codes = const.tile([P, PASSES, CHANNELS], U32, align_bytes=64)
        w_scales = const.tile([P, PASSES, CHANNELS], U8, align_bytes=64)
        x_codes = const.tile([P, PASSES, BATCH], U32, align_bytes=64)
        x_scales = const.tile([P, PASSES, BATCH], U8, align_bytes=64)

        group_rows, group_codes, group_scales = [], [], []
        for rows, codes, scales, count in (
            (w_rows, w_codes, w_scales, W_GROUPS),
            (x_rows, x_codes, x_scales, X_GROUPS),
        ):
            for n in range(count):
                group_rows.append(rows[:, n * GROUP : (n + 1) * GROUP, :])
                group_codes.append(codes[:, :, n * COLS : (n + 1) * COLS])
                group_scales.append(scales[:, :, n * COLS : (n + 1) * COLS])

        raw, norm, inverse, grouped, turned = {}, {}, {}, {}, {}

        def load(m):
            raw[m] = load_pool.tile([P, GROUP, K], BF16, name="raw")
            for i in range(GROUP):
                nc.sync.dma_start(out=raw[m][:, i, :], in_=group_rows[m][:, i, :])

        def row_norms(m):
            sumsq = small.tile([P, GROUP], F32)
            for i in range(GROUP):
                squares = scratch.tile([P, K], BF16)
                if m == 0 and i % 2 == 1:
                    nc.vector.scalar_tensor_tensor(
                        out=squares[:], in0=raw[m][:, i, :], scalar=1.0, in1=raw[m][:, i, :],
                        op0=ALU.mult, op1=ALU.mult, accum_out=sumsq[:, i : i + 1],
                    )
                else:
                    nc.scalar.activation(
                        out=squares[:], in_=raw[m][:, i, :], func=ACT.Square,
                        accum_out=sumsq[:, i : i + 1],
                    )
            norm[m] = small.tile([P, GROUP], F32, name="norm")
            nc.scalar.sqrt(out=norm[m][:], in_=sumsq[:])

        def invert(m):
            nc.vector.tensor_scalar(
                out=norm[m][:], in0=norm[m][:], scalar1=0.0, scalar2=EPS, op0=ALU.max, op1=ALU.add
            )
            inverse[m] = small.tile([P, GROUP], F32, name="inverse")
            nc.vector.reciprocal(out=inverse[m][:], in_=norm[m][:])

        def turn(m):
            unit = prep_pool.tile([P, GROUP * K], BF16)
            unit_words = unit[:].bitcast(F32)
            for i in range(GROUP):
                nc.vector.tensor_scalar_mul(
                    out=unit[:, i * K : (i + 1) * K].rearrange("p (u c e) -> p u c e", u=2, e=2),
                    in0=raw[m][:, i, :].rearrange("p (c u e) -> p u c e", u=2, e=2),
                    scalar1=inverse[m][:, i : i + 1],
                )
                turned[m, i] = turn_pool.tile([P, PASSES * 2, P], F32, name="turned", tag="turn")
                for s in range(PASSES * 2):
                    g, u = divmod(s, 2)
                    first = i * WORDS + (u * PASSES + g) * P
                    nc.tensor.transpose(
                        turned[m, i][:, s, :],
                        unit_words[:, first : first + P],
                        identity[:],
                    )

        def regroup(m):
            grouped[m] = prep_pool.tile(
                [P, PASSES * COLS * PACK], BF16, name="grouped", align_bytes=64
            )
            words = grouped[m][:].bitcast(F32).rearrange("p (g c u) -> p g c u", g=PASSES, u=2)
            for i in range(GROUP):
                copy = nc.scalar.copy if i == GROUP - 1 else nc.vector.tensor_copy
                copy(
                    out=words[:, :, i * P : (i + 1) * P, :],
                    in_=turned[m, i][:].rearrange("p (g u) r -> p g r u", u=2),
                )

        def quantise(m):
            for g in range(PASSES):
                nc.vector.quantize_mx(
                    out=group_codes[m][:, g, :].bitcast(FP8X4),
                    scales=group_scales[m][:, g, :],
                    in_=grouped[m][:, g * COLS * PACK : (g + 1) * COLS * PACK],
                )

        for m in range(-LOAD_AHEAD, GROUPS + 1):
            if 0 <= m + LOAD_AHEAD < GROUPS:
                load(m + LOAD_AHEAD)
            if 0 <= m < GROUPS:
                turn(m)
            if 0 <= m - 1 < GROUPS:
                quantise(m - 1)
            if 0 <= m < GROUPS:
                regroup(m)
            if 0 <= m + 1 < GROUPS:
                invert(m + 1)
            if 0 <= m + 2 < GROUPS:
                row_norms(m + 2)

        nc.sync.dma_start(out=gain_shift_rows[0:C_TILES, :], in_=g1.rearrange("(t p) -> t p", p=P))
        nc.sync.dma_start(
            out=gain_shift_rows[C_TILES : 2 * C_TILES, :], in_=b1.rearrange("(t p) -> t p", p=P)
        )
        gain_shift_turned = turn_pool.tile([P, P], BF16, tag="turn")
        nc.tensor.transpose(gain_shift_turned[:], gain_shift_rows[:], identity_bf16[:])
        gain_shift = const.tile([P, 2 * C_TILES], F32)
        nc.vector.tensor_copy(out=gain_shift[:], in_=gain_shift_turned[:, 0 : 2 * C_TILES])

        sims, partial, sums, minus_mean, spread, scale, offset = {}, {}, {}, {}, {}, {}, {}

        def similarities(k):
            u, q = divmod(k, PAIR_STEPS)
            if q == 0:
                partial[u] = small.tile([P, 2, PAIR, X_GROUPS], F32, name="partial")
            sims[k] = sims_pool.tile([P, PAIR, STEP_COLS], F32, name="sims")
            for h in range(STEP_GROUPS):
                n = q * STEP_GROUPS + h
                cols = slice(n * COLS, (n + 1) * COLS)
                for j in range(PAIR):
                    channels = slice((u * PAIR + j) * P, (u * PAIR + j + 1) * P)
                    product = product_pool.tile([P, COLS], F32)
                    for g in range(PASSES):
                        nc.tensor.matmul_mx(
                            out=product[:],
                            lhsT=w_codes[:, g, channels].bitcast(FP8X4),
                            lhsT_scale=w_scales[:, g, channels],
                            rhs=x_codes[:, g, cols].bitcast(FP8X4),
                            rhs_scale=x_scales[:, g, cols],
                            start=(g == 0),
                            stop=(g == PASSES - 1),
                        )
                    clipped = sims[k][:, j, h * COLS : (h + 1) * COLS]
                    nc.vector.scalar_tensor_tensor(
                        out=clipped, in0=product[:], scalar=0.0, in1=ones[:],
                        op0=ALU.max, op1=ALU.min, accum_out=partial[u][:, 0, j, n : n + 1],
                    )
                    squares = scratch.tile([P, COLS], BF16)
                    nc.scalar.activation(
                        out=squares[:], in_=clipped, func=ACT.Square,
                        accum_out=partial[u][:, 1, j, n : n + 1],
                    )

        def deviation(u):
            sums[u] = small.tile([P, 2, PAIR], F32, name="sums")
            nc.vector.tensor_reduce(out=sums[u][:], in_=partial[u][:], axis=AXIS.X, op=ALU.add)
            minus_mean[u] = small.tile([P, PAIR], F32, name="minus_mean")
            nc.scalar.activation(
                out=minus_mean[u][:], in_=sums[u][:, 0, :], func=ACT.Copy, scale=-1.0 / BATCH
            )
            squared_sum = small.tile([P, PAIR], F32)
            nc.scalar.activation(
                out=squared_sum[:], in_=sums[u][:, 0, :], func=ACT.Square, scale=BATCH**-0.5
            )
            spread[u] = small.tile([P, PAIR], F32, name="spread")
            for j in range(PAIR):
                nc.scalar.activation(
                    out=spread[u][:, j : j + 1], in_=squared_sum[:, j : j + 1], func=ACT.Relu,
                    scale=-1.0, bias=sums[u][:, 1, j : j + 1],
                )
            nc.scalar.activation(
                out=spread[u][:], in_=spread[u][:], func=ACT.Sqrt, scale=1.0 / BATCH, bias=bn_eps[:]
            )

        def scale_and_offset(u):
            nc.vector.reciprocal(out=spread[u][:], in_=spread[u][:])
            scale[u] = small.tile([P, PAIR], F32, name="scale")
            offset[u] = small.tile([P, PAIR], F32, name="offset")
            for j in range(PAIR):
                t = u * PAIR + j
                nc.scalar.activation(
                    out=scale[u][:, j : j + 1], in_=gain_shift[:, t : t + 1], func=ACT.Copy,
                    scale=spread[u][:, j : j + 1],
                )
            for j in range(PAIR):
                t = u * PAIR + j
                nc.scalar.activation(
                    out=offset[u][:, j : j + 1], in_=scale[u][:, j : j + 1], func=ACT.Identity,
                    scale=minus_mean[u][:, j : j + 1],
                    bias=gain_shift[:, C_TILES + t : C_TILES + t + 1],
                )

        def normalise(k):
            u, q = divmod(k, PAIR_STEPS)
            for j in range(PAIR):
                if u == C_TILES // PAIR - 2 and q == PAIR_STEPS - 1:
                    nc.scalar.activation(
                        out=sims[k][:, j, :], in_=sims[k][:, j, :], func=ACT.Identity,
                        scale=scale[u][:, j : j + 1], bias=offset[u][:, j : j + 1],
                    )
                    continue
                engine = nc.gpsimd if 0 < k < STEPS - PAIR_STEPS else nc.vector
                engine.tensor_scalar(
                    out=sims[k][:, j, :], in0=sims[k][:, j, :],
                    scalar1=scale[u][:, j : j + 1], scalar2=offset[u][:, j : j + 1],
                    op0=ALU.mult, op1=ALU.add,
                )

        def turn_back(k):
            u, q = divmod(k, PAIR_STEPS)
            stage = stage_pool.tile([P, STEP_TILES, PAIR * P], F32)
            for b in range(STEP_TILES // 2):
                flipped = turn_pool.tile([P, 2, PAIR, P], F32, tag="turn")
                for i in range(2):
                    images = slice((2 * b + i) * P, (2 * b + i + 1) * P)
                    for j in range(PAIR):
                        nc.tensor.transpose(flipped[:, i, j, :], sims[k][:, j, images], identity[:])
                staged = stage[:, 2 * b : 2 * b + 2, :]
                if b % 2 == 0:
                    nc.vector.tensor_copy(out=staged, in_=flipped[:].rearrange("p i j c -> p i (j c)"))
                else:
                    nc.scalar.copy(out=staged, in_=flipped[:].rearrange("p i j c -> p i (j c)"))
                if b % 2 == 1:
                    tiles = slice(2 * b - 2, 2 * b + 2)
                    nc.sync.dma_start(
                        out=out_rows[
                            :, q * STEP_TILES + 2 * b - 2 : q * STEP_TILES + 2 * b + 2,
                            u * PAIR * P : (u + 1) * PAIR * P,
                        ],
                        in_=stage[:, tiles, :],
                    )

        for k in range(STEPS + LAG):
            pair_done = k % PAIR_STEPS == 0 and k > 0 and k <= STEPS
            if k < STEPS:
                similarities(k)
            if pair_done:
                with tc.high_priority():
                    deviation(k // PAIR_STEPS - 1)
                    scale_and_offset(k // PAIR_STEPS - 1)
                    if k == PAIR_STEPS:
                        normalise(0)
                        turn_back(0)
            if k > LAG:
                turn_back(k - LAG)
            if 0 < k - LAG + 1 < STEPS:
                normalise(k - LAG + 1)
